import numpy as np
import ml_dtypes

BF16 = ml_dtypes.bfloat16


def bf(x):
    return np.asarray(x, np.float32).astype(BF16)


def f32(x):
    return np.asarray(x, np.float32)


def f64(x):
    return np.asarray(x).astype(np.float64)


def striped(idx):
    return np.tile(idx.reshape(-1, 16).T, (8, 1))


C, S, N = 512, 4096, 1536
EDGE_P = 0.02
GAIN = 4.0
BIAS = 0.2


def setup_inputs():
    x = bf(np.random.standard_normal((C, N)))
    adjacency = bf((np.random.random((N, N)) < EDGE_P) * (1.0 - np.eye(N)))
    W1 = bf(GAIN * np.random.standard_normal((C, C)) / np.sqrt(C))
    b1 = f32(BIAS * np.random.standard_normal((C, 1)))
    W2 = bf(GAIN * np.random.standard_normal((C, C)) / np.sqrt(C))
    b2 = f32(BIAS * np.random.standard_normal((C, 1)))
    base = f32(np.random.standard_normal((C, S)))
    return {"x": x, "adjacency": adjacency, "W1": W1, "b1": b1, "W2": W2, "b2": b2, "base": base, "offs": striped(np.random.permutation(S)[:N])}


def reference(x, adjacency, W1, b1, W2, b2, base, offs):
    idx = offs[:16].T.reshape(-1)
    ahat = f64(adjacency) + np.eye(N)
    deg = ahat.sum(axis=0)
    dinv = 1.0 / np.sqrt(deg)
    p1 = dinv[:, None] * (f64(x).T @ f64(W1))
    h1 = np.maximum(dinv[None, :] * (p1.T @ ahat) + f64(b1), 0.0)
    p2 = dinv[:, None] * (h1.T @ f64(W2))
    u = p2.T @ ahat
    t = np.maximum(u + f64(b2) * np.sqrt(deg)[None, :], 0.0)
    out = f64(base).copy()
    out[:, idx] = t * dinv[None, :]
    return out

@@ -1,0 +1,151 @@
+import concourse.mybir as mybir
+from concourse.masks import make_identity
+
+BF16 = mybir.dt.bfloat16
+F32 = mybir.dt.float32
+U16 = mybir.dt.uint16
+ADD = mybir.AluOpType.add
+MULT = mybir.AluOpType.mult
+FUNC = mybir.ActivationFunctionType
+
+P = 128
+C = 512
+S = 4096
+N = 1536
+BANK = 512
+CB = C // P
+NB = N // P
+NCH = N // BANK
+
+FLOPS = 2 * (2 * N * C * C + 2 * C * N * N)
+
+
+def tile_simplegcn_b_kernel(tc, x, adjacency, W1, b1, W2, b2, base, offs, out):
+    nc = tc.nc
+    with (
+        tc.tile_pool(name="held", bufs=1) as held,
+        tc.tile_pool(name="work", bufs=3) as work,
+        tc.psum_pool(name="banks", bufs=8) as banks,
+    ):
+        offsets = held.tile([P, N // 16], U16, name="offsets")
+        nc.sync.dma_start(offsets[:], offs)
+
+        ahat = [held.tile([P, N], BF16, name=f"ahat{ib}") for ib in range(NB)]
+        for ib in range(NB):
+            queue = nc.sync if ib % 2 == 0 else nc.scalar
+            queue.dma_start(ahat[ib][:], adjacency[ib * P : (ib + 1) * P, :])
+
+        w1_sb = held.tile([P, CB, C], BF16, name="w1_sb")
+        nc.sync.dma_start(w1_sb[:], W1.rearrange("(k p) c -> p k c", p=P))
+        x_sb = held.tile([P, CB, N], BF16, name="x_sb")
+        nc.scalar.dma_start(x_sb[:], x.rearrange("(k p) n -> p k n", p=P))
+
+        b1_col = held.tile([P, CB], F32, name="b1_col")
+        b2_col = held.tile([P, CB], F32, name="b2_col")
+        with nc.allow_non_contiguous_dma(reason="512 biases, one to a partition"):
+            nc.gpsimd.dma_start(b1_col[:], b1.rearrange("(k p) o -> p (k o)", p=P))
+            nc.gpsimd.dma_start(b2_col[:], b2.rearrange("(k p) o -> p (k o)", p=P))
+
+        w2_sb = held.tile([P, CB, C], BF16, name="w2_sb")
+        nc.sync.dma_start(w2_sb[:], W2.rearrange("(k p) c -> p k c", p=P))
+
+        window = [held.tile([P, S], F32, name=f"window{cb}") for cb in range(CB)]
+        for cb in range(CB):
+            queue = nc.sync if cb % 2 == 0 else nc.scalar
+            queue.dma_start(window[cb][:], base[cb * P : (cb + 1) * P, :])
+
+        ident_f32 = held.tile([P, P], F32, name="ident_f32")
+        make_identity(nc, ident_f32[:])
+        ident_bf = held.tile([P, P], BF16, name="ident_bf")
+        nc.vector.tensor_copy(ident_bf[:], ident_f32[:])
+        ones_bf = held.tile([P, P], BF16, name="ones_bf")
+        nc.vector.memset(ones_bf[:], 1.0)
+
+        for ib in range(NB):
+            diagonal = ahat[ib][:, ib * P : (ib + 1) * P]
+            nc.vector.tensor_tensor(diagonal, diagonal, ident_bf[:], ADD)
+
+        deg_ps = [banks.tile([P, BANK], F32, name=f"deg_ps{ch}", tag="bank") for ch in range(NCH)]
+        for ib in range(NB):
+            for ch in range(NCH):
+                nc.tensor.matmul(
+                    deg_ps[ch][:],
+                    ones_bf[:],
+                    ahat[ib][:, ch * BANK : (ch + 1) * BANK],
+                    start=(ib == 0),
+                    stop=(ib == NB - 1),
+                )
+
+        sqrtdeg_row = held.tile([P, N], F32, name="sqrtdeg_row")
+        for ch in range(NCH):
+            nc.scalar.activation(sqrtdeg_row[:, ch * BANK : (ch + 1) * BANK], deg_ps[ch][:], FUNC.Sqrt)
+
+        masked = held.tile([P, NB, P], F32, name="masked")
+        nc.vector.tensor_tensor(
+            masked[:],
+            sqrtdeg_row[:].rearrange("p (b q) -> p b q", q=P),
+            ident_f32[:].unsqueeze(1).to_broadcast([P, NB, P]),
+            MULT,
+        )
+        sqrtdeg_col = held.tile([P, NB], F32, name="sqrtdeg_col")
+        nc.vector.tensor_reduce(sqrtdeg_col[:], masked[:], mybir.AxisListType.X, ADD)
+        dinv_col = held.tile([P, NB], F32, name="dinv_col")
+        nc.vector.reciprocal(dinv_col[:], sqrtdeg_col[:])
+
+        dinv_row = held.tile([P, N], F32, name="dinv_row")
+        for ch in range(NCH):
+            chunk = slice(ch * BANK, (ch + 1) * BANK)
+            nc.vector.reciprocal(dinv_row[:, chunk], sqrtdeg_row[:, chunk])
+
+        def project(features, weights, name):
+            p_sb = []
+            for ib in range(NB):
+                q_ps = banks.tile([P, C], F32, name="q_ps", tag="bank")
+                for k in range(CB):
+                    nc.tensor.matmul(
+                        q_ps[:],
+                        features[:, k, ib * P : (ib + 1) * P],
+                        weights[:, k, :],
+                        start=(k == 0),
+                        stop=(k == CB - 1),
+                    )
+                p_ib = held.tile([P, C], BF16, name=f"{name}_{ib}")
+                nc.scalar.activation(p_ib[:], q_ps[:], FUNC.Copy, scale=dinv_col[:, ib : ib + 1])
+                p_sb.append(p_ib)
+            return p_sb
+
+        def aggregate(p_sb, cb, ch):
+            a_ps = banks.tile([P, BANK], F32, name="a_ps", tag="bank")
+            for ib in range(NB):
+                nc.tensor.matmul(
+                    a_ps[:],
+                    p_sb[ib][:, cb * P : (cb + 1) * P],
+                    ahat[ib][:, ch * BANK : (ch + 1) * BANK],
+                    start=(ib == 0),
+                    stop=(ib == NB - 1),
+                )
+            return a_ps
+
+        p1 = project(x_sb, w1_sb, "p1")
+        h1 = held.tile([P, CB, N], BF16, name="h1")
+        for ch in range(NCH):
+            chunk = slice(ch * BANK, (ch + 1) * BANK)
+            for cb in range(CB):
+                a_ps = aggregate(p1, cb, ch)
+                scaled = work.tile([P, BANK], F32, name="scaled")
+                nc.vector.tensor_tensor(scaled[:], a_ps[:], dinv_row[:, chunk], MULT)
+                nc.scalar.activation(h1[:, cb, chunk], scaled[:], FUNC.Relu, bias=b1_col[:, cb : cb + 1])
+
+        p2 = project(h1, w2_sb, "p2")
+        for cb in range(CB):
+            t = work.tile([P, N], F32, name="t", bufs=2)
+            for ch in range(NCH):
+                chunk = slice(ch * BANK, (ch + 1) * BANK)
+                u_ps = aggregate(p2, cb, ch)
+                biased = work.tile([P, BANK], F32, name="biased")
+                nc.vector.scalar_tensor_tensor(
+                    biased[:], sqrtdeg_row[:, chunk], b2_col[:, cb : cb + 1], u_ps[:], MULT, ADD
+                )
+                nc.scalar.activation(t[:, chunk], biased[:], FUNC.Relu)
+            nc.vector.tensor_tensor(window[cb][:].indirect(offsets[:]), t[:], dinv_row[:], MULT)
+            nc.sync.dma_start(out[cb * P : (cb + 1) * P, :], window[cb][:])

@@ -97,6 +97,10 @@ def tile_simplegcn_b_kernel(tc, x, adjacency, W1, b1, W2, b2, base, offs, out):
             chunk = slice(ch * BANK, (ch + 1) * BANK)
             nc.vector.reciprocal(dinv_row[:, chunk], sqrtdeg_row[:, chunk])
 
+        bias2 = [held.tile([P, N], F32, name=f"bias2_{cb}") for cb in range(CB)]
+        for cb in range(CB):
+            nc.vector.tensor_scalar_mul(bias2[cb][:], sqrtdeg_row[:], b2_col[:, cb : cb + 1])
+
         def project(features, weights, name):
             p_sb = []
             for ib in range(NB):
@@ -142,10 +146,10 @@ def tile_simplegcn_b_kernel(tc, x, adjacency, W1, b1, W2, b2, base, offs, out):
             for ch in range(NCH):
                 chunk = slice(ch * BANK, (ch + 1) * BANK)
                 u_ps = aggregate(p2, cb, ch)
+                u_sb = work.tile([P, BANK], F32, name="u_sb")
+                nc.scalar.copy(u_sb[:], u_ps[:])
                 biased = work.tile([P, BANK], F32, name="biased")
-                nc.vector.scalar_tensor_tensor(
-                    biased[:], sqrtdeg_row[:, chunk], b2_col[:, cb : cb + 1], u_ps[:], MULT, ADD
-                )
+                nc.gpsimd.tensor_tensor(biased[:], u_sb[:], bias2[cb][:, chunk], ADD)
                 nc.scalar.activation(t[:, chunk], biased[:], FUNC.Relu)
             nc.vector.tensor_tensor(window[cb][:].indirect(offsets[:]), t[:], dinv_row[:], MULT)
             nc.sync.dma_start(out[cb * P : (cb + 1) * P, :], window[cb][:])

@@ -16,6 +16,7 @@ BANK = 512
 CB = C // P
 NB = N // P
 NCH = N // BANK
+PER_BANK = BANK // P
 
 FLOPS = 2 * (2 * N * C * C + 2 * C * N * N)
 
@@ -97,10 +98,6 @@ def tile_simplegcn_b_kernel(tc, x, adjacency, W1, b1, W2, b2, base, offs, out):
             chunk = slice(ch * BANK, (ch + 1) * BANK)
             nc.vector.reciprocal(dinv_row[:, chunk], sqrtdeg_row[:, chunk])
 
-        bias2 = [held.tile([P, N], F32, name=f"bias2_{cb}") for cb in range(CB)]
-        for cb in range(CB):
-            nc.vector.tensor_scalar_mul(bias2[cb][:], sqrtdeg_row[:], b2_col[:, cb : cb + 1])
-
         def project(features, weights, name):
             p_sb = []
             for ib in range(NB):
@@ -118,12 +115,12 @@ def tile_simplegcn_b_kernel(tc, x, adjacency, W1, b1, W2, b2, base, offs, out):
                 p_sb.append(p_ib)
             return p_sb
 
-        def aggregate(p_sb, cb, ch):
+        def aggregate(p_blocks, ch):
             a_ps = banks.tile([P, BANK], F32, name="a_ps", tag="bank")
             for ib in range(NB):
                 nc.tensor.matmul(
                     a_ps[:],
-                    p_sb[ib][:, cb * P : (cb + 1) * P],
+                    p_blocks[ib],
                     ahat[ib][:, ch * BANK : (ch + 1) * BANK],
                     start=(ib == 0),
                     stop=(ib == NB - 1),
@@ -135,21 +132,37 @@ def tile_simplegcn_b_kernel(tc, x, adjacency, W1, b1, W2, b2, base, offs, out):
         for ch in range(NCH):
             chunk = slice(ch * BANK, (ch + 1) * BANK)
             for cb in range(CB):
-                a_ps = aggregate(p1, cb, ch)
+                a_ps = aggregate([p1[ib][:, cb * P : (cb + 1) * P] for ib in range(NB)], ch)
                 scaled = work.tile([P, BANK], F32, name="scaled")
                 nc.vector.tensor_tensor(scaled[:], a_ps[:], dinv_row[:, chunk], MULT)
                 nc.scalar.activation(h1[:, cb, chunk], scaled[:], FUNC.Relu, bias=b1_col[:, cb : cb + 1])
 
-        p2 = project(h1, w2_sb, "p2")
         for cb in range(CB):
+            p2 = work.tile([P, NB, P], BF16, name="p2", bufs=2)
+            for first in range(0, NB, PER_BANK):
+                group = range(first, first + PER_BANK)
+                q_ps = banks.tile([P, PER_BANK, P], F32, name="q2_ps", tag="bank")
+                for ib in group:
+                    for k in range(CB):
+                        nc.tensor.matmul(
+                            q_ps[:, ib - first, :],
+                            h1[:, k, ib * P : (ib + 1) * P],
+                            w2_sb[:, k, cb * P : (cb + 1) * P],
+                            start=(k == 0),
+                            stop=(k == CB - 1),
+                        )
+                for ib in group:
+                    nc.scalar.activation(
+                        p2[:, ib, :], q_ps[:, ib - first, :], FUNC.Copy, scale=dinv_col[:, ib : ib + 1]
+                    )
             t = work.tile([P, N], F32, name="t", bufs=2)
             for ch in range(NCH):
                 chunk = slice(ch * BANK, (ch + 1) * BANK)
-                u_ps = aggregate(p2, cb, ch)
-                u_sb = work.tile([P, BANK], F32, name="u_sb")
-                nc.scalar.copy(u_sb[:], u_ps[:])
+                u_ps = aggregate([p2[:, ib, :] for ib in range(NB)], ch)
                 biased = work.tile([P, BANK], F32, name="biased")
-                nc.gpsimd.tensor_tensor(biased[:], u_sb[:], bias2[cb][:, chunk], ADD)
+                nc.vector.scalar_tensor_tensor(
+                    biased[:], sqrtdeg_row[:, chunk], b2_col[:, cb : cb + 1], u_ps[:], MULT, ADD
+                )
                 nc.scalar.activation(t[:, chunk], biased[:], FUNC.Relu)
             nc.vector.tensor_tensor(window[cb][:].indirect(offsets[:]), t[:], dinv_row[:], MULT)
             nc.sync.dma_start(out[cb * P : (cb + 1) * P, :], window[cb][:])

@@ -28,18 +28,27 @@ def tile_simplegcn_b_kernel(tc, x, adjacency, W1, b1, W2, b2, base, offs, out):
         tc.tile_pool(name="work", bufs=3) as work,
         tc.psum_pool(name="banks", bufs=8) as banks,
     ):
+        ident_f32 = held.tile([P, P], F32, name="ident_f32")
+        make_identity(nc, ident_f32[:])
+        ident_bf = held.tile([P, P], BF16, name="ident_bf")
+        nc.vector.tensor_copy(ident_bf[:], ident_f32[:])
+        ones_bf = held.tile([P, P], BF16, name="ones_bf")
+        nc.vector.memset(ones_bf[:], 1.0)
+
         offsets = held.tile([P, N // 16], U16, name="offsets")
         nc.sync.dma_start(offsets[:], offs)
+
+        w1_sb = held.tile([P, CB, C], BF16, name="w1_sb")
+        x_sb = held.tile([P, CB, N], BF16, name="x_sb")
+        for k in range(CB):
+            queue = nc.sync if k % 2 == 0 else nc.scalar
+            queue.dma_start(w1_sb[:, k, :], W1[k * P : (k + 1) * P, :])
+            queue.dma_start(x_sb[:, k, :], x[k * P : (k + 1) * P, :])
 
         ahat = [held.tile([P, N], BF16, name=f"ahat{ib}") for ib in range(NB)]
         for ib in range(NB):
             queue = nc.sync if ib % 2 == 0 else nc.scalar
             queue.dma_start(ahat[ib][:], adjacency[ib * P : (ib + 1) * P, :])
-
-        w1_sb = held.tile([P, CB, C], BF16, name="w1_sb")
-        nc.sync.dma_start(w1_sb[:], W1.rearrange("(k p) c -> p k c", p=P))
-        x_sb = held.tile([P, CB, N], BF16, name="x_sb")
-        nc.scalar.dma_start(x_sb[:], x.rearrange("(k p) n -> p k n", p=P))
 
         b1_col = held.tile([P, CB], F32, name="b1_col")
         b2_col = held.tile([P, CB], F32, name="b2_col")
@@ -55,65 +64,50 @@ def tile_simplegcn_b_kernel(tc, x, adjacency, W1, b1, W2, b2, base, offs, out):
             queue = nc.sync if cb % 2 == 0 else nc.scalar
             queue.dma_start(window[cb][:], base[cb * P : (cb + 1) * P, :])
 
-        ident_f32 = held.tile([P, P], F32, name="ident_f32")
-        make_identity(nc, ident_f32[:])
-        ident_bf = held.tile([P, P], BF16, name="ident_bf")
-        nc.vector.tensor_copy(ident_bf[:], ident_f32[:])
-        ones_bf = held.tile([P, P], BF16, name="ones_bf")
-        nc.vector.memset(ones_bf[:], 1.0)
+        q1_sb = held.tile([P, NB, C], F32, name="q1_sb")
+        for ib in range(NB):
+            q_ps = banks.tile([P, C], F32, name="q1_ps", tag="bank")
+            for k in range(CB):
+                nc.tensor.matmul(
+                    q_ps[:],
+                    x_sb[:, k, ib * P : (ib + 1) * P],
+                    w1_sb[:, k, :],
+                    start=(k == 0),
+                    stop=(k == CB - 1),
+                )
+            nc.scalar.copy(q1_sb[:, ib, :], q_ps[:])
 
+        colsum = held.tile([P, N], BF16, name="colsum")
         for ib in range(NB):
             diagonal = ahat[ib][:, ib * P : (ib + 1) * P]
             nc.vector.tensor_tensor(diagonal, diagonal, ident_bf[:], ADD)
+            if ib == 0:
+                nc.vector.tensor_copy(colsum[:], ahat[ib][:])
+            else:
+                nc.vector.tensor_tensor(colsum[:], colsum[:], ahat[ib][:], ADD)
 
-        deg_ps = [banks.tile([P, BANK], F32, name=f"deg_ps{ch}", tag="bank") for ch in range(NCH)]
-        for ib in range(NB):
-            for ch in range(NCH):
-                nc.tensor.matmul(
-                    deg_ps[ch][:],
-                    ones_bf[:],
-                    ahat[ib][:, ch * BANK : (ch + 1) * BANK],
-                    start=(ib == 0),
-                    stop=(ib == NB - 1),
-                )
-
-        sqrtdeg_row = held.tile([P, N], F32, name="sqrtdeg_row")
-        for ch in range(NCH):
-            nc.scalar.activation(sqrtdeg_row[:, ch * BANK : (ch + 1) * BANK], deg_ps[ch][:], FUNC.Sqrt)
-
-        masked = held.tile([P, NB, P], F32, name="masked")
-        nc.vector.tensor_tensor(
-            masked[:],
-            sqrtdeg_row[:].rearrange("p (b q) -> p b q", q=P),
-            ident_f32[:].unsqueeze(1).to_broadcast([P, NB, P]),
-            MULT,
-        )
+        degcol_ps = banks.tile([P, NB], F32, name="degcol_ps", tag="bank")
+        for jb in range(NB):
+            nc.tensor.matmul(
+                degcol_ps[:, jb : jb + 1], colsum[:, jb * P : (jb + 1) * P], ones_bf[:, 0:1], start=True, stop=True
+            )
         sqrtdeg_col = held.tile([P, NB], F32, name="sqrtdeg_col")
-        nc.vector.tensor_reduce(sqrtdeg_col[:], masked[:], mybir.AxisListType.X, ADD)
+        nc.scalar.activation(sqrtdeg_col[:], degcol_ps[:], FUNC.Sqrt)
         dinv_col = held.tile([P, NB], F32, name="dinv_col")
         nc.vector.reciprocal(dinv_col[:], sqrtdeg_col[:])
 
+        p1 = [held.tile([P, C], BF16, name=f"p1_{ib}") for ib in range(NB)]
+        for ib in range(NB):
+            nc.vector.tensor_scalar_mul(p1[ib][:], q1_sb[:, ib, :], dinv_col[:, ib : ib + 1])
+
+        sqrtdeg_row = held.tile([P, N], F32, name="sqrtdeg_row")
         dinv_row = held.tile([P, N], F32, name="dinv_row")
         for ch in range(NCH):
             chunk = slice(ch * BANK, (ch + 1) * BANK)
+            deg_ps = banks.tile([P, BANK], F32, name="deg_ps", tag="bank")
+            nc.tensor.matmul(deg_ps[:], ones_bf[:], colsum[:, chunk], start=True, stop=True)
+            nc.scalar.activation(sqrtdeg_row[:, chunk], deg_ps[:], FUNC.Sqrt)
             nc.vector.reciprocal(dinv_row[:, chunk], sqrtdeg_row[:, chunk])
-
-        def project(features, weights, name):
-            p_sb = []
-            for ib in range(NB):
-                q_ps = banks.tile([P, C], F32, name="q_ps", tag="bank")
-                for k in range(CB):
-                    nc.tensor.matmul(
-                        q_ps[:],
-                        features[:, k, ib * P : (ib + 1) * P],
-                        weights[:, k, :],
-                        start=(k == 0),
-                        stop=(k == CB - 1),
-                    )
-                p_ib = held.tile([P, C], BF16, name=f"{name}_{ib}")
-                nc.scalar.activation(p_ib[:], q_ps[:], FUNC.Copy, scale=dinv_col[:, ib : ib + 1])
-                p_sb.append(p_ib)
-            return p_sb
 
         def aggregate(p_blocks, ch):
             a_ps = banks.tile([P, BANK], F32, name="a_ps", tag="bank")
@@ -127,7 +121,6 @@ def tile_simplegcn_b_kernel(tc, x, adjacency, W1, b1, W2, b2, base, offs, out):
                 )
             return a_ps
 
-        p1 = project(x_sb, w1_sb, "p1")
         h1 = held.tile([P, CB, N], BF16, name="h1")
         for ch in range(NCH):
             chunk = slice(ch * BANK, (ch + 1) * BANK)

@@ -41,14 +41,12 @@ def tile_simplegcn_b_kernel(tc, x, adjacency, W1, b1, W2, b2, base, offs, out):
         w1_sb = held.tile([P, CB, C], BF16, name="w1_sb")
         x_sb = held.tile([P, CB, N], BF16, name="x_sb")
         for k in range(CB):
-            queue = nc.sync if k % 2 == 0 else nc.scalar
-            queue.dma_start(w1_sb[:, k, :], W1[k * P : (k + 1) * P, :])
-            queue.dma_start(x_sb[:, k, :], x[k * P : (k + 1) * P, :])
+            nc.sync.dma_start(w1_sb[:, k, :], W1[k * P : (k + 1) * P, :])
+            nc.sync.dma_start(x_sb[:, k, :], x[k * P : (k + 1) * P, :])
 
         ahat = [held.tile([P, N], BF16, name=f"ahat{ib}") for ib in range(NB)]
         for ib in range(NB):
-            queue = nc.sync if ib % 2 == 0 else nc.scalar
-            queue.dma_start(ahat[ib][:], adjacency[ib * P : (ib + 1) * P, :])
+            nc.sync.dma_start(ahat[ib][:], adjacency[ib * P : (ib + 1) * P, :])
 
         b1_col = held.tile([P, CB], F32, name="b1_col")
         b2_col = held.tile([P, CB], F32, name="b2_col")
@@ -61,8 +59,7 @@ def tile_simplegcn_b_kernel(tc, x, adjacency, W1, b1, W2, b2, base, offs, out):
 
         window = [held.tile([P, S], F32, name=f"window{cb}") for cb in range(CB)]
         for cb in range(CB):
-            queue = nc.sync if cb % 2 == 0 else nc.scalar
-            queue.dma_start(window[cb][:], base[cb * P : (cb + 1) * P, :])
+            nc.sync.dma_start(window[cb][:], base[cb * P : (cb + 1) * P, :])
 
         q1_sb = held.tile([P, NB, C], F32, name="q1_sb")
         for ib in range(NB):

@@ -17,6 +17,7 @@ CB = C // P
 NB = N // P
 NCH = N // BANK
 PER_BANK = BANK // P
+GROUP = 4
 
 FLOPS = 2 * (2 * N * C * C + 2 * C * N * N)
 
@@ -34,77 +35,86 @@ def tile_simplegcn_b_kernel(tc, x, adjacency, W1, b1, W2, b2, base, offs, out):
         nc.vector.tensor_copy(ident_bf[:], ident_f32[:])
         ones_bf = held.tile([P, P], BF16, name="ones_bf")
         nc.vector.memset(ones_bf[:], 1.0)
+        warm = held.tile([P, 1], F32, name="warm")
+        nc.scalar.activation(warm[:], ones_bf[:, 0:1], FUNC.Sqrt)
 
         offsets = held.tile([P, N // 16], U16, name="offsets")
         nc.sync.dma_start(offsets[:], offs)
 
-        w1_sb = held.tile([P, CB, C], BF16, name="w1_sb")
-        x_sb = held.tile([P, CB, N], BF16, name="x_sb")
-        for k in range(CB):
-            nc.sync.dma_start(w1_sb[:, k, :], W1[k * P : (k + 1) * P, :])
-            nc.sync.dma_start(x_sb[:, k, :], x[k * P : (k + 1) * P, :])
-
         ahat = [held.tile([P, N], BF16, name=f"ahat{ib}") for ib in range(NB)]
-        for ib in range(NB):
-            nc.sync.dma_start(ahat[ib][:], adjacency[ib * P : (ib + 1) * P, :])
-
-        b1_col = held.tile([P, CB], F32, name="b1_col")
-        b2_col = held.tile([P, CB], F32, name="b2_col")
-        with nc.allow_non_contiguous_dma(reason="512 biases, one to a partition"):
-            nc.gpsimd.dma_start(b1_col[:], b1.rearrange("(k p) o -> p (k o)", p=P))
-            nc.gpsimd.dma_start(b2_col[:], b2.rearrange("(k p) o -> p (k o)", p=P))
-
-        w2_sb = held.tile([P, CB, C], BF16, name="w2_sb")
-        nc.sync.dma_start(w2_sb[:], W2.rearrange("(k p) c -> p k c", p=P))
-
-        window = [held.tile([P, S], F32, name=f"window{cb}") for cb in range(CB)]
-        for cb in range(CB):
-            nc.sync.dma_start(window[cb][:], base[cb * P : (cb + 1) * P, :])
-
-        q1_sb = held.tile([P, NB, C], F32, name="q1_sb")
-        for ib in range(NB):
-            q_ps = banks.tile([P, C], F32, name="q1_ps", tag="bank")
-            for k in range(CB):
-                nc.tensor.matmul(
-                    q_ps[:],
-                    x_sb[:, k, ib * P : (ib + 1) * P],
-                    w1_sb[:, k, :],
-                    start=(k == 0),
-                    stop=(k == CB - 1),
-                )
-            nc.scalar.copy(q1_sb[:, ib, :], q_ps[:])
-
-        colsum = held.tile([P, N], BF16, name="colsum")
-        for ib in range(NB):
-            diagonal = ahat[ib][:, ib * P : (ib + 1) * P]
-            nc.vector.tensor_tensor(diagonal, diagonal, ident_bf[:], ADD)
-            if ib == 0:
-                nc.vector.tensor_copy(colsum[:], ahat[ib][:])
-            else:
-                nc.vector.tensor_tensor(colsum[:], colsum[:], ahat[ib][:], ADD)
-
-        degcol_ps = banks.tile([P, NB], F32, name="degcol_ps", tag="bank")
-        for jb in range(NB):
-            nc.tensor.matmul(
-                degcol_ps[:, jb : jb + 1], colsum[:, jb * P : (jb + 1) * P], ones_bf[:, 0:1], start=True, stop=True
-            )
-        sqrtdeg_col = held.tile([P, NB], F32, name="sqrtdeg_col")
-        nc.scalar.activation(sqrtdeg_col[:], degcol_ps[:], FUNC.Sqrt)
-        dinv_col = held.tile([P, NB], F32, name="dinv_col")
-        nc.vector.reciprocal(dinv_col[:], sqrtdeg_col[:])
-
         p1 = [held.tile([P, C], BF16, name=f"p1_{ib}") for ib in range(NB)]
-        for ib in range(NB):
-            nc.vector.tensor_scalar_mul(p1[ib][:], q1_sb[:, ib, :], dinv_col[:, ib : ib + 1])
-
+        dinv_col = held.tile([P, NB], F32, name="dinv_col")
         sqrtdeg_row = held.tile([P, N], F32, name="sqrtdeg_row")
         dinv_row = held.tile([P, N], F32, name="dinv_row")
-        for ch in range(NCH):
-            chunk = slice(ch * BANK, (ch + 1) * BANK)
-            deg_ps = banks.tile([P, BANK], F32, name="deg_ps", tag="bank")
-            nc.tensor.matmul(deg_ps[:], ones_bf[:], colsum[:, chunk], start=True, stop=True)
-            nc.scalar.activation(sqrtdeg_row[:, chunk], deg_ps[:], FUNC.Sqrt)
-            nc.vector.reciprocal(dinv_row[:, chunk], sqrtdeg_row[:, chunk])
+        b1_col = held.tile([P, CB], F32, name="b1_col")
+        b2_col = held.tile([P, CB], F32, name="b2_col")
+        w2_sb = held.tile([P, CB, C], BF16, name="w2_sb")
+
+        with tc.tile_pool(name="first", bufs=1) as first_pool:
+            w1_sb = first_pool.tile([P, CB, C], BF16, name="w1_sb")
+            x_sb = first_pool.tile([P, CB, N], BF16, name="x_sb")
+            for k in range(CB):
+                nc.sync.dma_start(w1_sb[:, k, :], W1[k * P : (k + 1) * P, :])
+                nc.sync.dma_start(x_sb[:, k, :], x[k * P : (k + 1) * P, :])
+            for ib in range(NB):
+                nc.sync.dma_start(ahat[ib][:], adjacency[ib * P : (ib + 1) * P, :])
+            with nc.allow_non_contiguous_dma(reason="512 biases, one to a partition"):
+                nc.gpsimd.dma_start(b1_col[:], b1.rearrange("(k p) o -> p (k o)", p=P))
+                nc.gpsimd.dma_start(b2_col[:], b2.rearrange("(k p) o -> p (k o)", p=P))
+            nc.sync.dma_start(w2_sb[:], W2.rearrange("(k p) c -> p k c", p=P))
+
+            q1_sb = first_pool.tile([P, NB, C], F32, name="q1_sb")
+            for first in range(0, NB, GROUP):
+                group = range(first, first + GROUP)
+                q_ps = [banks.tile([P, C], F32, name=f"q1_ps{ib}", tag="bank") for ib in group]
+                for k in range(CB):
+                    for ib in group:
+                        nc.tensor.matmul(
+                            q_ps[ib - first][:],
+                            x_sb[:, k, ib * P : (ib + 1) * P],
+                            w1_sb[:, k, :],
+                            start=(k == 0),
+                            stop=(k == CB - 1),
+                        )
+                for ib in group:
+                    nc.scalar.copy(q1_sb[:, ib, :], q_ps[ib - first][:])
+
+            colsum = [first_pool.tile([P, N], BF16, name=f"colsum{half}") for half in range(2)]
+            for ib in range(NB):
+                if ib < 2:
+                    nc.vector.tensor_copy(colsum[ib][:], ahat[ib][:])
+                else:
+                    nc.vector.tensor_tensor(colsum[ib % 2][:], colsum[ib % 2][:], ahat[ib][:], ADD)
+
+            degcol_ps = banks.tile([P, NB], F32, name="degcol_ps", tag="bank")
+            for jb in range(NB):
+                for half in range(2):
+                    nc.tensor.matmul(
+                        degcol_ps[:, jb : jb + 1],
+                        colsum[half][:, jb * P : (jb + 1) * P],
+                        ones_bf[:, 0:1],
+                        start=(half == 0),
+                        stop=(half == 1),
+                    )
+            sqrtdeg_col = first_pool.tile([P, NB], F32, name="sqrtdeg_col")
+            nc.scalar.activation(sqrtdeg_col[:], degcol_ps[:], FUNC.Sqrt, bias=1.0)
+            nc.vector.reciprocal(dinv_col[:], sqrtdeg_col[:])
+
+            for ib in range(NB):
+                if ib % 2 == 0:
+                    nc.vector.tensor_scalar_mul(p1[ib][:], q1_sb[:, ib, :], dinv_col[:, ib : ib + 1])
+                else:
+                    nc.scalar.activation(p1[ib][:], q1_sb[:, ib, :], FUNC.Copy, scale=dinv_col[:, ib : ib + 1])
+
+            for ch in range(NCH):
+                chunk = slice(ch * BANK, (ch + 1) * BANK)
+                deg_ps = banks.tile([P, BANK], F32, name="deg_ps", tag="bank")
+                for half in range(2):
+                    nc.tensor.matmul(
+                        deg_ps[:], ones_bf[:], colsum[half][:, chunk], start=(half == 0), stop=(half == 1)
+                    )
+                nc.scalar.activation(sqrtdeg_row[:, chunk], deg_ps[:], FUNC.Sqrt, bias=1.0)
+                nc.vector.reciprocal(dinv_row[:, chunk], sqrtdeg_row[:, chunk])
 
         def aggregate(p_blocks, ch):
             a_ps = banks.tile([P, BANK], F32, name="a_ps", tag="bank")
@@ -118,41 +128,50 @@ def tile_simplegcn_b_kernel(tc, x, adjacency, W1, b1, W2, b2, base, offs, out):
                 )
             return a_ps
 
-        h1 = held.tile([P, CB, N], BF16, name="h1")
-        for ch in range(NCH):
-            chunk = slice(ch * BANK, (ch + 1) * BANK)
-            for cb in range(CB):
-                a_ps = aggregate([p1[ib][:, cb * P : (cb + 1) * P] for ib in range(NB)], ch)
-                scaled = work.tile([P, BANK], F32, name="scaled")
-                nc.vector.tensor_tensor(scaled[:], a_ps[:], dinv_row[:, chunk], MULT)
-                nc.scalar.activation(h1[:, cb, chunk], scaled[:], FUNC.Relu, bias=b1_col[:, cb : cb + 1])
-
-        for cb in range(CB):
-            p2 = work.tile([P, NB, P], BF16, name="p2", bufs=2)
-            for first in range(0, NB, PER_BANK):
-                group = range(first, first + PER_BANK)
-                q_ps = banks.tile([P, PER_BANK, P], F32, name="q2_ps", tag="bank")
-                for ib in group:
-                    for k in range(CB):
-                        nc.tensor.matmul(
-                            q_ps[:, ib - first, :],
-                            h1[:, k, ib * P : (ib + 1) * P],
-                            w2_sb[:, k, cb * P : (cb + 1) * P],
-                            start=(k == 0),
-                            stop=(k == CB - 1),
-                        )
-                for ib in group:
-                    nc.scalar.activation(
-                        p2[:, ib, :], q_ps[:, ib - first, :], FUNC.Copy, scale=dinv_col[:, ib : ib + 1]
-                    )
-            t = work.tile([P, N], F32, name="t", bufs=2)
+        with tc.tile_pool(name="store", bufs=2) as store:
+            h1 = held.tile([P, CB, N], BF16, name="h1")
             for ch in range(NCH):
                 chunk = slice(ch * BANK, (ch + 1) * BANK)
-                u_ps = aggregate([p2[:, ib, :] for ib in range(NB)], ch)
-                biased = work.tile([P, BANK], F32, name="biased")
-                nc.vector.scalar_tensor_tensor(
-                    biased[:], sqrtdeg_row[:, chunk], b2_col[:, cb : cb + 1], u_ps[:], MULT, ADD
-                )
-                nc.scalar.activation(t[:, chunk], biased[:], FUNC.Relu)
-            nc.vector.tensor_tensor(window[cb][:].indirect(offsets[:]), t[:], dinv_row[:], MULT)
-            nc.sync.dma_start(out[cb * P : (cb + 1) * P, :], window[cb][:])
+                for ib in range(ch * PER_BANK, (ch + 1) * PER_BANK):
+                    diagonal = ahat[ib][:, ib * P : (ib + 1) * P]
+                    nc.vector.tensor_tensor(diagonal, diagonal, ident_bf[:], ADD)
+                for cb in range(CB):
+                    a_ps = aggregate([p1[ib][:, cb * P : (cb + 1) * P] for ib in range(NB)], ch)
+                    scaled = work.tile([P, BANK], F32, name="scaled")
+                    nc.vector.tensor_tensor(scaled[:], a_ps[:], dinv_row[:, chunk], MULT)
+                    nc.scalar.activation(h1[:, cb, chunk], scaled[:], FUNC.Relu, bias=b1_col[:, cb : cb + 1])
+
+            for cb in range(CB):
+                window = store.tile([P, S], F32, name="window")
+                nc.sync.dma_start(window[:], base[cb * P : (cb + 1) * P, :])
+
+                p2 = work.tile([P, NB, P], BF16, name="p2", bufs=2)
+                for first in range(0, NB, PER_BANK):
+                    group = range(first, first + PER_BANK)
+                    q_ps = banks.tile([P, PER_BANK, P], F32, name="q2_ps", tag="bank")
+                    for ib in group:
+                        for k in range(CB):
+                            nc.tensor.matmul(
+                                q_ps[:, ib - first, :],
+                                h1[:, k, ib * P : (ib + 1) * P],
+                                w2_sb[:, k, cb * P : (cb + 1) * P],
+                                start=(k == 0),
+                                stop=(k == CB - 1),
+                            )
+                    for ib in group:
+                        nc.scalar.activation(
+                            p2[:, ib, :], q_ps[:, ib - first, :], FUNC.Copy, scale=dinv_col[:, ib : ib + 1]
+                        )
+
+                t = work.tile([P, N], F32, name="t", bufs=2)
+                for ch in range(NCH):
+                    chunk = slice(ch * BANK, (ch + 1) * BANK)
+                    u_ps = aggregate([p2[:, ib, :] for ib in range(NB)], ch)
+                    biased = work.tile([P, BANK], F32, name="biased")
+                    nc.vector.scalar_tensor_tensor(
+                        biased[:], sqrtdeg_row[:, chunk], b2_col[:, cb : cb + 1], u_ps[:], MULT, ADD
+                    )
+                    nc.scalar.activation(t[:, chunk], biased[:], FUNC.Relu)
+
+                nc.vector.tensor_tensor(window[:].indirect(offsets[:]), t[:], dinv_row[:], MULT)
+                nc.sync.dma_start(out[cb * P : (cb + 1) * P, :], window[:])

@@ -163,7 +163,6 @@ def tile_simplegcn_b_kernel(tc, x, adjacency, W1, b1, W2, b2, base, offs, out):
                             p2[:, ib, :], q_ps[:, ib - first, :], FUNC.Copy, scale=dinv_col[:, ib : ib + 1]
                         )
 
-                t = work.tile([P, N], F32, name="t", bufs=2)
                 for ch in range(NCH):
                     chunk = slice(ch * BANK, (ch + 1) * BANK)
                     u_ps = aggregate([p2[:, ib, :] for ib in range(NB)], ch)
@@ -171,7 +170,8 @@ def tile_simplegcn_b_kernel(tc, x, adjacency, W1, b1, W2, b2, base, offs, out):
                     nc.vector.scalar_tensor_tensor(
                         biased[:], sqrtdeg_row[:, chunk], b2_col[:, cb : cb + 1], u_ps[:], MULT, ADD
                     )
-                    nc.scalar.activation(t[:, chunk], biased[:], FUNC.Relu)
-
-                nc.vector.tensor_tensor(window[:].indirect(offsets[:]), t[:], dinv_row[:], MULT)
+                    t = work.tile([P, BANK], F32, name="t")
+                    nc.scalar.activation(t[:], biased[:], FUNC.Relu)
+                    piece = offsets[:, ch * BANK // 16 : (ch + 1) * BANK // 16]
+                    nc.vector.tensor_tensor(window[:].indirect(piece), t[:], dinv_row[:, chunk], MULT)
                 nc.sync.dma_start(out[cb * P : (cb + 1) * P, :], window[:])

@@ -171,7 +171,7 @@ def tile_simplegcn_b_kernel(tc, x, adjacency, W1, b1, W2, b2, base, offs, out):
                         biased[:], sqrtdeg_row[:, chunk], b2_col[:, cb : cb + 1], u_ps[:], MULT, ADD
                     )
                     t = work.tile([P, BANK], F32, name="t")
-                    nc.scalar.activation(t[:], biased[:], FUNC.Relu)
+                    nc.vector.tensor_scalar_max(t[:], biased[:], 0.0)
                     piece = offsets[:, ch * BANK // 16 : (ch + 1) * BANK // 16]
                     nc.vector.tensor_tensor(window[:].indirect(piece), t[:], dinv_row[:, chunk], MULT)
                 nc.sync.dma_start(out[cb * P : (cb + 1) * P, :], window[:])

@@ -128,7 +128,7 @@ def tile_simplegcn_b_kernel(tc, x, adjacency, W1, b1, W2, b2, base, offs, out):
                 )
             return a_ps
 
-        with tc.tile_pool(name="store", bufs=2) as store:
+        with tc.tile_pool(name="store", bufs=CB) as store:
             h1 = held.tile([P, CB, N], BF16, name="h1")
             for ch in range(NCH):
                 chunk = slice(ch * BANK, (ch + 1) * BANK)

@@ -163,15 +163,22 @@ def tile_simplegcn_b_kernel(tc, x, adjacency, W1, b1, W2, b2, base, offs, out):
                             p2[:, ib, :], q_ps[:, ib - first, :], FUNC.Copy, scale=dinv_col[:, ib : ib + 1]
                         )
 
-                for ch in range(NCH):
-                    chunk = slice(ch * BANK, (ch + 1) * BANK)
-                    u_ps = aggregate([p2[:, ib, :] for ib in range(NB)], ch)
-                    biased = work.tile([P, BANK], F32, name="biased")
-                    nc.vector.scalar_tensor_tensor(
-                        biased[:], sqrtdeg_row[:, chunk], b2_col[:, cb : cb + 1], u_ps[:], MULT, ADD
-                    )
-                    t = work.tile([P, BANK], F32, name="t")
+                for chunks in (range(0, 1), range(1, NCH)):
+                    nodes = slice(chunks.start * BANK, chunks.stop * BANK)
+                    biased = work.tile([P, len(chunks) * BANK], F32, name=f"biased{len(chunks)}", bufs=2)
+                    for ch in chunks:
+                        chunk = slice(ch * BANK, (ch + 1) * BANK)
+                        u_ps = aggregate([p2[:, ib, :] for ib in range(NB)], ch)
+                        nc.vector.scalar_tensor_tensor(
+                            biased[:, (ch - chunks.start) * BANK : (ch - chunks.start + 1) * BANK],
+                            sqrtdeg_row[:, chunk],
+                            b2_col[:, cb : cb + 1],
+                            u_ps[:],
+                            MULT,
+                            ADD,
+                        )
+                    t = work.tile([P, len(chunks) * BANK], F32, name=f"t{len(chunks)}", bufs=2)
                     nc.vector.tensor_scalar_max(t[:], biased[:], 0.0)
-                    piece = offsets[:, ch * BANK // 16 : (ch + 1) * BANK // 16]
-                    nc.vector.tensor_tensor(window[:].indirect(piece), t[:], dinv_row[:, chunk], MULT)
+                    piece = offsets[:, chunks.start * BANK // 16 : chunks.stop * BANK // 16]
+                    nc.vector.tensor_tensor(window[:].indirect(piece), t[:], dinv_row[:, nodes], MULT)
                 nc.sync.dma_start(out[cb * P : (cb + 1) * P, :], window[:])

@@ -165,20 +165,19 @@ def tile_simplegcn_b_kernel(tc, x, adjacency, W1, b1, W2, b2, base, offs, out):
 
                 for chunks in (range(0, 1), range(1, NCH)):
                     nodes = slice(chunks.start * BANK, chunks.stop * BANK)
-                    biased = work.tile([P, len(chunks) * BANK], F32, name=f"biased{len(chunks)}", bufs=2)
+                    t = work.tile([P, len(chunks) * BANK], F32, name=f"t{len(chunks)}", bufs=2)
                     for ch in chunks:
                         chunk = slice(ch * BANK, (ch + 1) * BANK)
                         u_ps = aggregate([p2[:, ib, :] for ib in range(NB)], ch)
+                        biased = work.tile([P, BANK], F32, name="biased")
                         nc.vector.scalar_tensor_tensor(
-                            biased[:, (ch - chunks.start) * BANK : (ch - chunks.start + 1) * BANK],
-                            sqrtdeg_row[:, chunk],
-                            b2_col[:, cb : cb + 1],
-                            u_ps[:],
-                            MULT,
-                            ADD,
+                            biased[:], sqrtdeg_row[:, chunk], b2_col[:, cb : cb + 1], u_ps[:], MULT, ADD
                         )
-                    t = work.tile([P, len(chunks) * BANK], F32, name=f"t{len(chunks)}", bufs=2)
-                    nc.vector.tensor_scalar_max(t[:], biased[:], 0.0)
+                        t_chunk = t[:, (ch - chunks.start) * BANK : (ch - chunks.start + 1) * BANK]
+                        if ch == chunks.stop - 1:
+                            nc.vector.tensor_scalar_max(t_chunk, biased[:], 0.0)
+                        else:
+                            nc.scalar.activation(t_chunk, biased[:], FUNC.Relu)
                     piece = offsets[:, chunks.start * BANK // 16 : chunks.stop * BANK // 16]
                     nc.vector.tensor_tensor(window[:].indirect(piece), t[:], dinv_row[:, nodes], MULT)
                 nc.sync.dma_start(out[cb * P : (cb + 1) * P, :], window[:])

import concourse.mybir as mybir
from concourse.masks import make_identity

BF16 = mybir.dt.bfloat16
F32 = mybir.dt.float32
U16 = mybir.dt.uint16
ADD = mybir.AluOpType.add
MULT = mybir.AluOpType.mult
FUNC = mybir.ActivationFunctionType

P = 128
C = 512
S = 4096
N = 1536
BANK = 512
CB = C // P
NB = N // P
NCH = N // BANK
PER_BANK = BANK // P
GROUP = 4

FLOPS = 2 * (2 * N * C * C + 2 * C * N * N)


def tile_simplegcn_b_kernel(tc, x, adjacency, W1, b1, W2, b2, base, offs, out):
    nc = tc.nc
    with (
        tc.tile_pool(name="held", bufs=1) as held,
        tc.tile_pool(name="work", bufs=3) as work,
        tc.psum_pool(name="banks", bufs=8) as banks,
    ):
        ident_f32 = held.tile([P, P], F32, name="ident_f32")
        make_identity(nc, ident_f32[:])
        ident_bf = held.tile([P, P], BF16, name="ident_bf")
        nc.vector.tensor_copy(ident_bf[:], ident_f32[:])
        ones_bf = held.tile([P, P], BF16, name="ones_bf")
        nc.vector.memset(ones_bf[:], 1.0)
        warm = held.tile([P, 1], F32, name="warm")
        nc.scalar.activation(warm[:], ones_bf[:, 0:1], FUNC.Sqrt)

        offsets = held.tile([P, N // 16], U16, name="offsets")
        nc.sync.dma_start(offsets[:], offs)

        ahat = [held.tile([P, N], BF16, name=f"ahat{ib}") for ib in range(NB)]
        p1 = [held.tile([P, C], BF16, name=f"p1_{ib}") for ib in range(NB)]
        dinv_col = held.tile([P, NB], F32, name="dinv_col")
        sqrtdeg_row = held.tile([P, N], F32, name="sqrtdeg_row")
        dinv_row = held.tile([P, N], F32, name="dinv_row")
        b1_col = held.tile([P, CB], F32, name="b1_col")
        b2_col = held.tile([P, CB], F32, name="b2_col")
        w2_sb = held.tile([P, CB, C], BF16, name="w2_sb")

        with tc.tile_pool(name="first", bufs=1) as first_pool:
            w1_sb = first_pool.tile([P, CB, C], BF16, name="w1_sb")
            x_sb = first_pool.tile([P, CB, N], BF16, name="x_sb")
            for k in range(CB):
                nc.sync.dma_start(w1_sb[:, k, :], W1[k * P : (k + 1) * P, :])
                nc.sync.dma_start(x_sb[:, k, :], x[k * P : (k + 1) * P, :])
            for ib in range(NB):
                nc.sync.dma_start(ahat[ib][:], adjacency[ib * P : (ib + 1) * P, :])
            with nc.allow_non_contiguous_dma(reason="512 biases, one to a partition"):
                nc.gpsimd.dma_start(b1_col[:], b1.rearrange("(k p) o -> p (k o)", p=P))
                nc.gpsimd.dma_start(b2_col[:], b2.rearrange("(k p) o -> p (k o)", p=P))
            nc.sync.dma_start(w2_sb[:], W2.rearrange("(k p) c -> p k c", p=P))

            q1_sb = first_pool.tile([P, NB, C], F32, name="q1_sb")
            for first in range(0, NB, GROUP):
                group = range(first, first + GROUP)
                q_ps = [banks.tile([P, C], F32, name=f"q1_ps{ib}", tag="bank") for ib in group]
                for k in range(CB):
                    for ib in group:
                        nc.tensor.matmul(
                            q_ps[ib - first][:],
                            x_sb[:, k, ib * P : (ib + 1) * P],
                            w1_sb[:, k, :],
                            start=(k == 0),
                            stop=(k == CB - 1),
                        )
                for ib in group:
                    nc.scalar.copy(q1_sb[:, ib, :], q_ps[ib - first][:])

            colsum = [first_pool.tile([P, N], BF16, name=f"colsum{half}") for half in range(2)]
            for ib in range(NB):
                if ib < 2:
                    nc.vector.tensor_copy(colsum[ib][:], ahat[ib][:])
                else:
                    nc.vector.tensor_tensor(colsum[ib % 2][:], colsum[ib % 2][:], ahat[ib][:], ADD)

            degcol_ps = banks.tile([P, NB], F32, name="degcol_ps", tag="bank")
            for jb in range(NB):
                for half in range(2):
                    nc.tensor.matmul(
                        degcol_ps[:, jb : jb + 1],
                        colsum[half][:, jb * P : (jb + 1) * P],
                        ones_bf[:, 0:1],
                        start=(half == 0),
                        stop=(half == 1),
                    )
            sqrtdeg_col = first_pool.tile([P, NB], F32, name="sqrtdeg_col")
            nc.scalar.activation(sqrtdeg_col[:], degcol_ps[:], FUNC.Sqrt, bias=1.0)
            nc.vector.reciprocal(dinv_col[:], sqrtdeg_col[:])

            for ib in range(NB):
                if ib % 2 == 0:
                    nc.vector.tensor_scalar_mul(p1[ib][:], q1_sb[:, ib, :], dinv_col[:, ib : ib + 1])
                else:
                    nc.scalar.activation(p1[ib][:], q1_sb[:, ib, :], FUNC.Copy, scale=dinv_col[:, ib : ib + 1])

            for ch in range(NCH):
                chunk = slice(ch * BANK, (ch + 1) * BANK)
                deg_ps = banks.tile([P, BANK], F32, name="deg_ps", tag="bank")
                for half in range(2):
                    nc.tensor.matmul(
                        deg_ps[:], ones_bf[:], colsum[half][:, chunk], start=(half == 0), stop=(half == 1)
                    )
                nc.scalar.activation(sqrtdeg_row[:, chunk], deg_ps[:], FUNC.Sqrt, bias=1.0)
                nc.vector.reciprocal(dinv_row[:, chunk], sqrtdeg_row[:, chunk])

        def aggregate(p_blocks, ch):
            a_ps = banks.tile([P, BANK], F32, name="a_ps", tag="bank")
            for ib in range(NB):
                nc.tensor.matmul(
                    a_ps[:],
                    p_blocks[ib],
                    ahat[ib][:, ch * BANK : (ch + 1) * BANK],
                    start=(ib == 0),
                    stop=(ib == NB - 1),
                )
            return a_ps

        with tc.tile_pool(name="store", bufs=CB) as store:
            h1 = held.tile([P, CB, N], BF16, name="h1")
            for ch in range(NCH):
                chunk = slice(ch * BANK, (ch + 1) * BANK)
                for ib in range(ch * PER_BANK, (ch + 1) * PER_BANK):
                    diagonal = ahat[ib][:, ib * P : (ib + 1) * P]
                    nc.vector.tensor_tensor(diagonal, diagonal, ident_bf[:], ADD)
                for cb in range(CB):
                    a_ps = aggregate([p1[ib][:, cb * P : (cb + 1) * P] for ib in range(NB)], ch)
                    scaled = work.tile([P, BANK], F32, name="scaled")
                    nc.vector.tensor_tensor(scaled[:], a_ps[:], dinv_row[:, chunk], MULT)
                    nc.scalar.activation(h1[:, cb, chunk], scaled[:], FUNC.Relu, bias=b1_col[:, cb : cb + 1])

            for cb in range(CB):
                window = store.tile([P, S], F32, name="window")
                nc.sync.dma_start(window[:], base[cb * P : (cb + 1) * P, :])

                p2 = work.tile([P, NB, P], BF16, name="p2", bufs=2)
                for first in range(0, NB, PER_BANK):
                    group = range(first, first + PER_BANK)
                    q_ps = banks.tile([P, PER_BANK, P], F32, name="q2_ps", tag="bank")
                    for ib in group:
                        for k in range(CB):
                            nc.tensor.matmul(
                                q_ps[:, ib - first, :],
                                h1[:, k, ib * P : (ib + 1) * P],
                                w2_sb[:, k, cb * P : (cb + 1) * P],
                                start=(k == 0),
                                stop=(k == CB - 1),
                            )
                    for ib in group:
                        nc.scalar.activation(
                            p2[:, ib, :], q_ps[:, ib - first, :], FUNC.Copy, scale=dinv_col[:, ib : ib + 1]
                        )

                for chunks in (range(0, 1), range(1, NCH)):
                    nodes = slice(chunks.start * BANK, chunks.stop * BANK)
                    t = work.tile([P, len(chunks) * BANK], F32, name=f"t{len(chunks)}", bufs=2)
                    for ch in chunks:
                        chunk = slice(ch * BANK, (ch + 1) * BANK)
                        u_ps = aggregate([p2[:, ib, :] for ib in range(NB)], ch)
                        biased = work.tile([P, BANK], F32, name="biased")
                        nc.vector.scalar_tensor_tensor(
                            biased[:], sqrtdeg_row[:, chunk], b2_col[:, cb : cb + 1], u_ps[:], MULT, ADD
                        )
                        t_chunk = t[:, (ch - chunks.start) * BANK : (ch - chunks.start + 1) * BANK]
                        if ch == chunks.stop - 1:
                            nc.vector.tensor_scalar_max(t_chunk, biased[:], 0.0)
                        else:
                            nc.scalar.activation(t_chunk, biased[:], FUNC.Relu)
                    piece = offsets[:, chunks.start * BANK // 16 : chunks.stop * BANK // 16]
                    nc.vector.tensor_tensor(window[:].indirect(piece), t[:], dinv_row[:, nodes], MULT)
                nc.sync.dma_start(out[cb * P : (cb + 1) * P, :], window[:])
